import numpy as np
import ml_dtypes


def mxq(x, axis, fmt="e4m3"):
    dtype, down = {"e4m3": (ml_dtypes.float8_e4m3fn, 7), "e5m2": (ml_dtypes.float8_e5m2, 14)}[fmt]
    v = np.moveaxis(np.asarray(x, np.float32).astype(ml_dtypes.bfloat16).astype(np.float64), axis, -1)
    blocks = v.reshape(v.shape[:-1] + (-1, 32))
    amax = np.abs(blocks).max(-1, keepdims=True)
    byte = np.maximum(np.where(amax > 0, np.frexp(amax)[1] - 1 + 127, 0) - down, 1)
    scale = np.exp2(byte - 127.0)
    codes = (blocks / scale).astype(np.float32).astype(dtype).astype(np.float64)
    return np.moveaxis((codes * scale).reshape(v.shape), -1, axis)


WIDE = False


def mx_kscale(k):
    if not WIDE:
        return np.ones(k)
    levels = np.array([10, -10, 5, -5, 0])
    a = np.random.permutation(np.resize(levels, k // 512 * 4)).reshape(k // 512, 4)
    idx = np.arange(k)
    return np.exp2(a[idx // 512, idx % 128 // 32])


BF16 = ml_dtypes.bfloat16


def bf(x):
    return np.asarray(x, np.float32).astype(BF16)


def f64(x):
    return np.asarray(x).astype(np.float64)


N, B, T, C, R, O, NC, H, W = 31, 128, 4, 256, 4, 512, 512, 16, 4
K = C * R
LEAKY_SLOPE = 0.01


def setup_inputs():
    s = mx_kscale(K)
    return {"pooled": bf((0.65 + 0.3 * np.random.standard_normal((N, B, K))) * s),
            "p": bf(0.65 + 0.5 * np.random.standard_normal((N, B, T, C))),
            "Wout": bf((4.0 / np.sqrt(K) * np.random.standard_normal((N, K, C)) - 4.0 / K) / s[None, :, None])}


def reference(pooled, p, Wout):
    y = mxq(f64(pooled), 2, "e4m3") @ mxq(f64(Wout), 1, "e4m3")
    y = np.where(y >= 0, y, LEAKY_SLOPE * y)
    return np.max(f64(p) + y[:, :, None, :], axis=2)

@@ -1,0 +1,198 @@
+import concourse.mybir as mybir
+from concourse.masks import make_identity
+
+BF16 = mybir.dt.bfloat16
+F32 = mybir.dt.float32
+U32 = mybir.dt.uint32
+U8 = mybir.dt.uint8
+FP8X4 = mybir.dt.float8_e4m3fn_x4
+MAX = mybir.AluOpType.max
+ADD = mybir.AluOpType.add
+
+BINS = 31
+SAMPLES = 128
+FRAMES = 4
+CHANNELS = 256
+K = 1024
+LEAKY_SLOPE = 0.01
+
+P = 128
+PACK = 4
+K_PASS = P * PACK
+PASSES = K // K_PASS
+PAIR = 2
+WORDS = PACK // PAIR
+
+GROUP = 2
+ROUNDS = (BINS + GROUP - 1) // GROUP
+UNITS = GROUP * PASSES
+
+RUN = 4
+W_COLS_SCALAR = 176
+
+FLOPS = 2 * BINS * SAMPLES * K * CHANNELS
+
+
+def tile_gmpahead_pa_kernel(tc, pooled, p, Wout, out):
+    nc = tc.nc
+
+    with tc.tile_pool(name="const", bufs=1) as const, tc.tile_pool(
+        name="loads", bufs=4
+    ) as loads, tc.tile_pool(name="work", bufs=3) as work, tc.tile_pool(
+        name="late", bufs=4
+    ) as late, tc.psum_pool(name="xt_banks", bufs=4) as xt_banks, tc.psum_pool(
+        name="y_banks", bufs=3
+    ) as y_banks:
+        identity = const.tile([P, P], F32)
+        make_identity(nc, identity[:])
+
+        kept = {}
+
+        def bins_of(r):
+            first = r * GROUP
+            return first, min(GROUP, BINS - first)
+
+        def prepare(r):
+            first, nb = bins_of(r)
+            units = nb * PASSES
+
+            x_raw = loads.tile([P, GROUP * K], BF16)
+            nc.sync.dma_start(
+                out=x_raw[:, : nb * K].rearrange("b (n k) -> b n k", n=nb),
+                in_=pooled[first : first + nb].rearrange("n b k -> b n k"),
+            )
+            w_raw = loads.tile([P, UNITS * PACK * CHANNELS], BF16)
+            nc.sync.dma_start(
+                out=w_raw[:, : units * PACK * CHANNELS].rearrange("q (s f) -> q s f", s=units),
+                in_=Wout[first : first + nb].rearrange(
+                    "n (g q t) c -> q (n g) (t c)", g=PASSES, t=PACK
+                ),
+            )
+            p_raw = loads.tile([P, GROUP * FRAMES * CHANNELS], BF16)
+            nc.sync.dma_start(
+                out=p_raw[:, : nb * FRAMES * CHANNELS].rearrange("b (n f) -> b n f", n=nb),
+                in_=p[first : first + nb].rearrange("n b t c -> b n (t c)"),
+            )
+
+            x_words = x_raw[:].bitcast(F32).rearrange(
+                "b (n g q u) -> b n g u q", n=GROUP, g=PASSES, u=WORDS
+            )
+            x_grouped = work.tile([P, GROUP * K], BF16, align_bytes=64)
+            x_grouped_words = x_grouped[:].bitcast(F32).rearrange(
+                "q (n g b u) -> q n g b u", n=GROUP, g=PASSES, u=WORDS
+            )
+            x_turned = []
+            for n in range(nb):
+                xt = xt_banks.tile([P, PASSES, WORDS, SAMPLES], F32)
+                for g in range(PASSES):
+                    for u in range(WORDS):
+                        nc.tensor.transpose(xt[:, g, u, :], x_words[:, n, g, u, :], identity[:])
+                x_turned.append(xt)
+
+            w_grouped = work.tile([P, UNITS * CHANNELS * PACK], BF16, align_bytes=64)
+            w_from = w_raw[:].rearrange("q (s t c i) -> q s c t i", s=UNITS, t=PACK, i=RUN)
+            w_to = w_grouped[:].rearrange("q (s c i t) -> q s c t i", s=UNITS, t=PACK, i=RUN)
+            split = W_COLS_SCALAR // RUN
+            for s in range(units):
+                nc.scalar.copy(out=w_to[:, s, :split], in_=w_from[:, s, :split])
+            nc.vector.tensor_copy(out=w_to[:, :units, split:], in_=w_from[:, :units, split:])
+
+            for n in range(nb):
+                nc.scalar.copy(
+                    out=x_grouped_words[:, n], in_=x_turned[n][:].rearrange("q g u b -> q g b u")
+                )
+
+            p_halves = p_raw[:].rearrange("b (n h f) -> b n h f", n=GROUP, h=2)
+            p_half = work.tile([P, GROUP * 2 * CHANNELS], BF16)
+            nc.vector.tensor_tensor(
+                out=p_half[:].rearrange("b (n f) -> b n f", n=GROUP)[:, :nb],
+                in0=p_halves[:, :nb, 0, :],
+                in1=p_halves[:, :nb, 1, :],
+                op=MAX,
+            )
+            kept[r] = {"x_grouped": x_grouped, "w_grouped": w_grouped, "p_half": p_half}
+
+        def multiply(r):
+            first, nb = bins_of(r)
+            units = nb * PASSES
+            mine = kept[r]
+
+            x_codes = work.tile([P, UNITS * SAMPLES], U32, align_bytes=64)
+            x_scales = work.tile([P, UNITS * SAMPLES], U8, align_bytes=64)
+            nc.vector.quantize_mx(
+                out=x_codes[:, : units * SAMPLES].bitcast(FP8X4),
+                scales=x_scales[:, : units * SAMPLES],
+                in_=mine["x_grouped"][:, : units * SAMPLES * PACK],
+            )
+            w_codes = work.tile([P, UNITS * CHANNELS], U32, align_bytes=64)
+            w_scales = work.tile([P, UNITS * CHANNELS], U8, align_bytes=64)
+            nc.vector.quantize_mx(
+                out=w_codes[:, : units * CHANNELS].bitcast(FP8X4),
+                scales=w_scales[:, : units * CHANNELS],
+                in_=mine["w_grouped"][:, : units * CHANNELS * PACK],
+            )
+
+            y = y_banks.tile([P, GROUP * CHANNELS], F32)
+            for n in range(nb):
+                for g in range(PASSES):
+                    s = n * PASSES + g
+                    x_cols = slice(s * SAMPLES, (s + 1) * SAMPLES)
+                    w_cols = slice(s * CHANNELS, (s + 1) * CHANNELS)
+                    nc.tensor.matmul_mx(
+                        out=y[:, n * CHANNELS : (n + 1) * CHANNELS],
+                        lhsT=x_codes[:, x_cols].bitcast(FP8X4),
+                        lhsT_scale=x_scales[:, x_cols],
+                        rhs=w_codes[:, w_cols].bitcast(FP8X4),
+                        rhs_scale=w_scales[:, w_cols],
+                        start=(g == 0),
+                        stop=(g == PASSES - 1),
+                    )
+
+            p_pairs = mine["p_half"][:].rearrange("b (n h c) -> b n h c", n=GROUP, h=2)
+            p_max = late.tile([P, GROUP * CHANNELS], BF16)
+            nc.vector.tensor_tensor(
+                out=p_max[:].rearrange("b (n c) -> b n c", n=GROUP)[:, :nb],
+                in0=p_pairs[:, :nb, 0, :],
+                in1=p_pairs[:, :nb, 1, :],
+                op=MAX,
+            )
+
+            y_small = late.tile([P, GROUP * CHANNELS], F32)
+            nc.scalar.mul(
+                out=y_small[:, : nb * CHANNELS], in_=y[:, : nb * CHANNELS], mul=LEAKY_SLOPE
+            )
+            kept[r] = {"y": y, "y_small": y_small, "p_max": p_max}
+
+        def relu(r):
+            first, nb = bins_of(r)
+            mine = kept[r]
+            y_leaky = late.tile([P, GROUP * CHANNELS], F32)
+            nc.vector.tensor_tensor(
+                out=y_leaky[:, : nb * CHANNELS],
+                in0=mine["y"][:, : nb * CHANNELS],
+                in1=mine["y_small"][:, : nb * CHANNELS],
+                op=MAX,
+            )
+            kept[r] = {"y_leaky": y_leaky, "p_max": mine["p_max"]}
+
+        def finish(r):
+            first, nb = bins_of(r)
+            mine = kept[r]
+            feat = late.tile([P, GROUP * CHANNELS], F32)
+            nc.vector.tensor_tensor(
+                out=feat[:, : nb * CHANNELS],
+                in0=mine["y_leaky"][:, : nb * CHANNELS],
+                in1=mine["p_max"][:, : nb * CHANNELS],
+                op=ADD,
+            )
+            nc.gpsimd.dma_start(
+                out=out[first : first + nb].rearrange("n b c -> b n c"),
+                in_=feat[:, : nb * CHANNELS].rearrange("b (n c) -> b n c", n=nb),
+            )
+
+        stages = [prepare, multiply, relu, finish]
+        with tc.manual_schedule():
+            for step in range(ROUNDS + len(stages) - 1):
+                for lag, stage in enumerate(stages):
+                    if 0 <= step - lag < ROUNDS:
+                        stage(step - lag)

@@ -30,6 +30,9 @@ UNITS = GROUP * PASSES
 RUN = 4
 W_COLS_SCALAR = 176
 
+AHEAD = 2
+P_LATER = 2
+
 FLOPS = 2 * BINS * SAMPLES * K * CHANNELS
 
 
@@ -37,12 +40,10 @@ def tile_gmpahead_pa_kernel(tc, pooled, p, Wout, out):
     nc = tc.nc
 
     with tc.tile_pool(name="const", bufs=1) as const, tc.tile_pool(
-        name="loads", bufs=4
-    ) as loads, tc.tile_pool(name="work", bufs=3) as work, tc.tile_pool(
-        name="late", bufs=4
-    ) as late, tc.psum_pool(name="xt_banks", bufs=4) as xt_banks, tc.psum_pool(
-        name="y_banks", bufs=3
-    ) as y_banks:
+        name="loads", bufs=AHEAD + 2
+    ) as loads, tc.tile_pool(name="work", bufs=3) as work, tc.psum_pool(
+        name="xt_banks", bufs=4
+    ) as xt_banks, tc.psum_pool(name="y_banks", bufs=3) as y_banks:
         identity = const.tile([P, P], F32)
         make_identity(nc, identity[:])
 
@@ -52,10 +53,9 @@ def tile_gmpahead_pa_kernel(tc, pooled, p, Wout, out):
             first = r * GROUP
             return first, min(GROUP, BINS - first)
 
-        def prepare(r):
+        def fetch_operands(r):
             first, nb = bins_of(r)
             units = nb * PASSES
-
             x_raw = loads.tile([P, GROUP * K], BF16)
             nc.sync.dma_start(
                 out=x_raw[:, : nb * K].rearrange("b (n k) -> b n k", n=nb),
@@ -68,68 +68,66 @@ def tile_gmpahead_pa_kernel(tc, pooled, p, Wout, out):
                     "n (g q t) c -> q (n g) (t c)", g=PASSES, t=PACK
                 ),
             )
+            kept[r] = {"x_raw": x_raw, "w_raw": w_raw}
+
+        def fetch_frames(r):
+            first, nb = bins_of(r)
             p_raw = loads.tile([P, GROUP * FRAMES * CHANNELS], BF16)
             nc.sync.dma_start(
                 out=p_raw[:, : nb * FRAMES * CHANNELS].rearrange("b (n f) -> b n f", n=nb),
                 in_=p[first : first + nb].rearrange("n b t c -> b n (t c)"),
             )
+            kept[r]["p_raw"] = p_raw
 
-            x_words = x_raw[:].bitcast(F32).rearrange(
+        def prepare(r):
+            first, nb = bins_of(r)
+            units = nb * PASSES
+
+            x_words = kept[r]["x_raw"][:].bitcast(F32).rearrange(
                 "b (n g q u) -> b n g u q", n=GROUP, g=PASSES, u=WORDS
             )
             x_grouped = work.tile([P, GROUP * K], BF16, align_bytes=64)
             x_grouped_words = x_grouped[:].bitcast(F32).rearrange(
                 "q (n g b u) -> q n g b u", n=GROUP, g=PASSES, u=WORDS
             )
-            x_turned = []
             for n in range(nb):
                 xt = xt_banks.tile([P, PASSES, WORDS, SAMPLES], F32)
                 for g in range(PASSES):
                     for u in range(WORDS):
                         nc.tensor.transpose(xt[:, g, u, :], x_words[:, n, g, u, :], identity[:])
-                x_turned.append(xt)
+                nc.scalar.copy(
+                    out=x_grouped_words[:, n], in_=xt[:].rearrange("q g u b -> q g b u")
+                )
 
             w_grouped = work.tile([P, UNITS * CHANNELS * PACK], BF16, align_bytes=64)
-            w_from = w_raw[:].rearrange("q (s t c i) -> q s c t i", s=UNITS, t=PACK, i=RUN)
+            w_from = kept[r]["w_raw"][:].rearrange(
+                "q (s t c i) -> q s c t i", s=UNITS, t=PACK, i=RUN
+            )
             w_to = w_grouped[:].rearrange("q (s c i t) -> q s c t i", s=UNITS, t=PACK, i=RUN)
             split = W_COLS_SCALAR // RUN
             for s in range(units):
                 nc.scalar.copy(out=w_to[:, s, :split], in_=w_from[:, s, :split])
             nc.vector.tensor_copy(out=w_to[:, :units, split:], in_=w_from[:, :units, split:])
-
-            for n in range(nb):
-                nc.scalar.copy(
-                    out=x_grouped_words[:, n], in_=x_turned[n][:].rearrange("q g u b -> q g b u")
-                )
-
-            p_halves = p_raw[:].rearrange("b (n h f) -> b n h f", n=GROUP, h=2)
-            p_half = work.tile([P, GROUP * 2 * CHANNELS], BF16)
-            nc.vector.tensor_tensor(
-                out=p_half[:].rearrange("b (n f) -> b n f", n=GROUP)[:, :nb],
-                in0=p_halves[:, :nb, 0, :],
-                in1=p_halves[:, :nb, 1, :],
-                op=MAX,
-            )
-            kept[r] = {"x_grouped": x_grouped, "w_grouped": w_grouped, "p_half": p_half}
+            kept[r]["x_grouped"] = x_grouped
+            kept[r]["w_grouped"] = w_grouped
 
         def multiply(r):
             first, nb = bins_of(r)
             units = nb * PASSES
-            mine = kept[r]
 
             x_codes = work.tile([P, UNITS * SAMPLES], U32, align_bytes=64)
             x_scales = work.tile([P, UNITS * SAMPLES], U8, align_bytes=64)
             nc.vector.quantize_mx(
                 out=x_codes[:, : units * SAMPLES].bitcast(FP8X4),
                 scales=x_scales[:, : units * SAMPLES],
-                in_=mine["x_grouped"][:, : units * SAMPLES * PACK],
+                in_=kept[r]["x_grouped"][:, : units * SAMPLES * PACK],
             )
             w_codes = work.tile([P, UNITS * CHANNELS], U32, align_bytes=64)
             w_scales = work.tile([P, UNITS * CHANNELS], U8, align_bytes=64)
             nc.vector.quantize_mx(
                 out=w_codes[:, : units * CHANNELS].bitcast(FP8X4),
                 scales=w_scales[:, : units * CHANNELS],
-                in_=mine["w_grouped"][:, : units * CHANNELS * PACK],
+                in_=kept[r]["w_grouped"][:, : units * CHANNELS * PACK],
             )
 
             y = y_banks.tile([P, GROUP * CHANNELS], F32)
@@ -148,51 +146,61 @@ def tile_gmpahead_pa_kernel(tc, pooled, p, Wout, out):
                         stop=(g == PASSES - 1),
                     )
 
-            p_pairs = mine["p_half"][:].rearrange("b (n h c) -> b n h c", n=GROUP, h=2)
-            p_max = late.tile([P, GROUP * CHANNELS], BF16)
+            y_small = work.tile([P, GROUP * CHANNELS], F32)
+            nc.scalar.mul(
+                out=y_small[:, : nb * CHANNELS], in_=y[:, : nb * CHANNELS], mul=LEAKY_SLOPE
+            )
+            kept[r]["y"] = y
+            kept[r]["y_small"] = y_small
+
+        def relu(r):
+            first, nb = bins_of(r)
+            cols = nb * CHANNELS
+
+            p_halves = kept[r]["p_raw"][:].rearrange("b (n h f) -> b n h f", n=GROUP, h=2)
+            p_half = work.tile([P, GROUP * 2 * CHANNELS], BF16)
+            nc.vector.tensor_tensor(
+                out=p_half[:].rearrange("b (n f) -> b n f", n=GROUP)[:, :nb],
+                in0=p_halves[:, :nb, 0, :],
+                in1=p_halves[:, :nb, 1, :],
+                op=MAX,
+            )
+            y_leaky = work.tile([P, GROUP * CHANNELS], F32)
+            nc.vector.tensor_tensor(
+                out=y_leaky[:, :cols], in0=kept[r]["y"][:, :cols], in1=kept[r]["y_small"][:, :cols], op=MAX
+            )
+            p_pairs = p_half[:].rearrange("b (n h c) -> b n h c", n=GROUP, h=2)
+            p_max = work.tile([P, GROUP * CHANNELS], BF16)
             nc.vector.tensor_tensor(
                 out=p_max[:].rearrange("b (n c) -> b n c", n=GROUP)[:, :nb],
                 in0=p_pairs[:, :nb, 0, :],
                 in1=p_pairs[:, :nb, 1, :],
                 op=MAX,
             )
-
-            y_small = late.tile([P, GROUP * CHANNELS], F32)
-            nc.scalar.mul(
-                out=y_small[:, : nb * CHANNELS], in_=y[:, : nb * CHANNELS], mul=LEAKY_SLOPE
-            )
-            kept[r] = {"y": y, "y_small": y_small, "p_max": p_max}
-
-        def relu(r):
-            first, nb = bins_of(r)
-            mine = kept[r]
-            y_leaky = late.tile([P, GROUP * CHANNELS], F32)
-            nc.vector.tensor_tensor(
-                out=y_leaky[:, : nb * CHANNELS],
-                in0=mine["y"][:, : nb * CHANNELS],
-                in1=mine["y_small"][:, : nb * CHANNELS],
-                op=MAX,
-            )
-            kept[r] = {"y_leaky": y_leaky, "p_max": mine["p_max"]}
+            kept[r]["y_leaky"] = y_leaky
+            kept[r]["p_max"] = p_max
 
         def finish(r):
             first, nb = bins_of(r)
-            mine = kept[r]
-            feat = late.tile([P, GROUP * CHANNELS], F32)
+            cols = nb * CHANNELS
+            feat = work.tile([P, GROUP * CHANNELS], F32)
             nc.vector.tensor_tensor(
-                out=feat[:, : nb * CHANNELS],
-                in0=mine["y_leaky"][:, : nb * CHANNELS],
-                in1=mine["p_max"][:, : nb * CHANNELS],
-                op=ADD,
+                out=feat[:, :cols], in0=kept[r]["y_leaky"][:, :cols], in1=kept[r]["p_max"][:, :cols], op=ADD
             )
-            nc.gpsimd.dma_start(
+            nc.sync.dma_start(
                 out=out[first : first + nb].rearrange("n b c -> b n c"),
-                in_=feat[:, : nb * CHANNELS].rearrange("b (n c) -> b n c", n=nb),
+                in_=feat[:, :cols].rearrange("b (n c) -> b n c", n=nb),
             )
 
-        stages = [prepare, multiply, relu, finish]
+        def run(stage, r):
+            if 0 <= r < ROUNDS:
+                stage(r)
+
         with tc.manual_schedule():
-            for step in range(ROUNDS + len(stages) - 1):
-                for lag, stage in enumerate(stages):
-                    if 0 <= step - lag < ROUNDS:
-                        stage(step - lag)
+            for step in range(ROUNDS + AHEAD + 3):
+                run(fetch_operands, step)
+                run(fetch_frames, step - P_LATER)
+                run(prepare, step - AHEAD)
+                run(multiply, step - AHEAD - 1)
+                run(relu, step - AHEAD - 2)
+                run(finish, step - AHEAD - 3)

@@ -3,6 +3,7 @@ from concourse.masks import make_identity
 
 BF16 = mybir.dt.bfloat16
 F32 = mybir.dt.float32
+I32 = mybir.dt.int32
 U32 = mybir.dt.uint32
 U8 = mybir.dt.uint8
 FP8X4 = mybir.dt.float8_e4m3fn_x4
@@ -27,6 +28,9 @@ GROUP = 2
 ROUNDS = (BINS + GROUP - 1) // GROUP
 UNITS = GROUP * PASSES
 
+X_SLOT = P * (GROUP - 1) + P // GROUP
+X_SETS = 2
+
 RUN = 4
 W_COLS_SCALAR = 176
 
@@ -38,14 +42,27 @@ FLOPS = 2 * BINS * SAMPLES * K * CHANNELS
 
 def tile_gmpahead_pa_kernel(tc, pooled, p, Wout, out):
     nc = tc.nc
+    pooled_rows = pooled.rearrange("n b k -> (n b) k")
+    p_rows = p.rearrange("n b t c -> (n b) (t c)")
+    out_rows = out.rearrange("n b c -> (n b) c")
 
     with tc.tile_pool(name="const", bufs=1) as const, tc.tile_pool(
         name="loads", bufs=AHEAD + 2
     ) as loads, tc.tile_pool(name="work", bufs=3) as work, tc.psum_pool(
-        name="xt_banks", bufs=4
+        name="xt_banks", bufs=2 * GROUP
     ) as xt_banks, tc.psum_pool(name="y_banks", bufs=3) as y_banks:
         identity = const.tile([P, P], F32)
         make_identity(nc, identity[:])
+
+        x_code_sets = []
+        x_scale_sets = []
+        for i in range(X_SETS):
+            x_codes = const.tile([P, UNITS * X_SLOT], U32, align_bytes=64, name="x_codes_%d" % i)
+            x_scales = const.tile([P, UNITS * X_SLOT], U8, align_bytes=64, name="x_scales_%d" % i)
+            nc.vector.memset(x_codes[:].bitcast(I32), 0)
+            nc.vector.memset(x_scales[:].bitcast(I32), 0)
+            x_code_sets.append(x_codes)
+            x_scale_sets.append(x_scales)
 
         kept = {}
 
@@ -53,14 +70,17 @@ def tile_gmpahead_pa_kernel(tc, pooled, p, Wout, out):
             first = r * GROUP
             return first, min(GROUP, BINS - first)
 
+        def rows_of(r, dram_rows):
+            first, nb = bins_of(r)
+            return dram_rows[first * SAMPLES : (first + nb) * SAMPLES, :].rearrange(
+                "(i j) w -> i (j w)", j=nb
+            )
+
         def fetch_operands(r):
             first, nb = bins_of(r)
             units = nb * PASSES
             x_raw = loads.tile([P, GROUP * K], BF16)
-            nc.sync.dma_start(
-                out=x_raw[:, : nb * K].rearrange("b (n k) -> b n k", n=nb),
-                in_=pooled[first : first + nb].rearrange("n b k -> b n k"),
-            )
+            nc.sync.dma_start(out=x_raw[:, : nb * K], in_=rows_of(r, pooled_rows))
             w_raw = loads.tile([P, UNITS * PACK * CHANNELS], BF16)
             nc.sync.dma_start(
                 out=w_raw[:, : units * PACK * CHANNELS].rearrange("q (s f) -> q s f", s=units),
@@ -73,10 +93,7 @@ def tile_gmpahead_pa_kernel(tc, pooled, p, Wout, out):
         def fetch_frames(r):
             first, nb = bins_of(r)
             p_raw = loads.tile([P, GROUP * FRAMES * CHANNELS], BF16)
-            nc.sync.dma_start(
-                out=p_raw[:, : nb * FRAMES * CHANNELS].rearrange("b (n f) -> b n f", n=nb),
-                in_=p[first : first + nb].rearrange("n b t c -> b n (t c)"),
-            )
+            nc.sync.dma_start(out=p_raw[:, : nb * FRAMES * CHANNELS], in_=rows_of(r, p_rows))
             kept[r]["p_raw"] = p_raw
 
         def prepare(r):
@@ -84,19 +101,19 @@ def tile_gmpahead_pa_kernel(tc, pooled, p, Wout, out):
             units = nb * PASSES
 
             x_words = kept[r]["x_raw"][:].bitcast(F32).rearrange(
-                "b (n g q u) -> b n g u q", n=GROUP, g=PASSES, u=WORDS
+                "i (j g q u) -> i j g u q", j=GROUP, g=PASSES, u=WORDS
             )
             x_grouped = work.tile([P, GROUP * K], BF16, align_bytes=64)
             x_grouped_words = x_grouped[:].bitcast(F32).rearrange(
-                "q (n g b u) -> q n g b u", n=GROUP, g=PASSES, u=WORDS
+                "q (j g i u) -> q j g i u", j=GROUP, g=PASSES, u=WORDS
             )
-            for n in range(nb):
-                xt = xt_banks.tile([P, PASSES, WORDS, SAMPLES], F32)
+            for j in range(nb):
+                xt = xt_banks.tile([P, PASSES, WORDS, P], F32)
                 for g in range(PASSES):
                     for u in range(WORDS):
-                        nc.tensor.transpose(xt[:, g, u, :], x_words[:, n, g, u, :], identity[:])
+                        nc.tensor.transpose(xt[:, g, u, :], x_words[:, j, g, u, :], identity[:])
                 nc.scalar.copy(
-                    out=x_grouped_words[:, n], in_=xt[:].rearrange("q g u b -> q g b u")
+                    out=x_grouped_words[:, j], in_=xt[:].rearrange("q g u i -> q g i u")
                 )
 
             w_grouped = work.tile([P, UNITS * CHANNELS * PACK], BF16, align_bytes=64)
@@ -114,14 +131,20 @@ def tile_gmpahead_pa_kernel(tc, pooled, p, Wout, out):
         def multiply(r):
             first, nb = bins_of(r)
             units = nb * PASSES
+            share = P // nb
 
-            x_codes = work.tile([P, UNITS * SAMPLES], U32, align_bytes=64)
-            x_scales = work.tile([P, UNITS * SAMPLES], U8, align_bytes=64)
-            nc.vector.quantize_mx(
-                out=x_codes[:, : units * SAMPLES].bitcast(FP8X4),
-                scales=x_scales[:, : units * SAMPLES],
-                in_=kept[r]["x_grouped"][:, : units * SAMPLES * PACK],
-            )
+            x_codes = x_code_sets[r % X_SETS]
+            x_scales = x_scale_sets[r % X_SETS]
+            for s in range(units):
+                for n in range(nb):
+                    filled = slice(s * X_SLOT + n * P, s * X_SLOT + n * P + share)
+                    nc.vector.quantize_mx(
+                        out=x_codes[:, filled].bitcast(FP8X4),
+                        scales=x_scales[:, filled],
+                        in_=kept[r]["x_grouped"][
+                            :, (s * P + n * share) * PACK : (s * P + (n + 1) * share) * PACK
+                        ],
+                    )
             w_codes = work.tile([P, UNITS * CHANNELS], U32, align_bytes=64)
             w_scales = work.tile([P, UNITS * CHANNELS], U8, align_bytes=64)
             nc.vector.quantize_mx(
@@ -131,20 +154,22 @@ def tile_gmpahead_pa_kernel(tc, pooled, p, Wout, out):
             )
 
             y = y_banks.tile([P, GROUP * CHANNELS], F32)
-            for n in range(nb):
-                for g in range(PASSES):
-                    s = n * PASSES + g
-                    x_cols = slice(s * SAMPLES, (s + 1) * SAMPLES)
-                    w_cols = slice(s * CHANNELS, (s + 1) * CHANNELS)
-                    nc.tensor.matmul_mx(
-                        out=y[:, n * CHANNELS : (n + 1) * CHANNELS],
-                        lhsT=x_codes[:, x_cols].bitcast(FP8X4),
-                        lhsT_scale=x_scales[:, x_cols],
-                        rhs=w_codes[:, w_cols].bitcast(FP8X4),
-                        rhs_scale=w_scales[:, w_cols],
-                        start=(g == 0),
-                        stop=(g == PASSES - 1),
-                    )
+            for j in range(nb):
+                for n in range(nb):
+                    for g in range(PASSES):
+                        x_start = (j * PASSES + g) * X_SLOT + n * share
+                        x_cols = slice(x_start, x_start + P)
+                        w_start = (n * PASSES + g) * CHANNELS
+                        w_cols = slice(w_start, w_start + CHANNELS)
+                        nc.tensor.matmul_mx(
+                            out=y[:, j * CHANNELS : (j + 1) * CHANNELS],
+                            lhsT=x_codes[:, x_cols].bitcast(FP8X4),
+                            lhsT_scale=x_scales[:, x_cols],
+                            rhs=w_codes[:, w_cols].bitcast(FP8X4),
+                            rhs_scale=w_scales[:, w_cols],
+                            start=(n == 0 and g == 0),
+                            stop=(n == nb - 1 and g == PASSES - 1),
+                        )
 
             y_small = work.tile([P, GROUP * CHANNELS], F32)
             nc.scalar.mul(
@@ -157,22 +182,25 @@ def tile_gmpahead_pa_kernel(tc, pooled, p, Wout, out):
             first, nb = bins_of(r)
             cols = nb * CHANNELS
 
-            p_halves = kept[r]["p_raw"][:].rearrange("b (n h f) -> b n h f", n=GROUP, h=2)
+            p_halves = kept[r]["p_raw"][:].rearrange("i (j h f) -> i j h f", j=GROUP, h=2)
             p_half = work.tile([P, GROUP * 2 * CHANNELS], BF16)
             nc.vector.tensor_tensor(
-                out=p_half[:].rearrange("b (n f) -> b n f", n=GROUP)[:, :nb],
+                out=p_half[:].rearrange("i (j f) -> i j f", j=GROUP)[:, :nb],
                 in0=p_halves[:, :nb, 0, :],
                 in1=p_halves[:, :nb, 1, :],
                 op=MAX,
             )
             y_leaky = work.tile([P, GROUP * CHANNELS], F32)
             nc.vector.tensor_tensor(
-                out=y_leaky[:, :cols], in0=kept[r]["y"][:, :cols], in1=kept[r]["y_small"][:, :cols], op=MAX
+                out=y_leaky[:, :cols],
+                in0=kept[r]["y"][:, :cols],
+                in1=kept[r]["y_small"][:, :cols],
+                op=MAX,
             )
-            p_pairs = p_half[:].rearrange("b (n h c) -> b n h c", n=GROUP, h=2)
+            p_pairs = p_half[:].rearrange("i (j h c) -> i j h c", j=GROUP, h=2)
             p_max = work.tile([P, GROUP * CHANNELS], BF16)
             nc.vector.tensor_tensor(
-                out=p_max[:].rearrange("b (n c) -> b n c", n=GROUP)[:, :nb],
+                out=p_max[:].rearrange("i (j c) -> i j c", j=GROUP)[:, :nb],
                 in0=p_pairs[:, :nb, 0, :],
                 in1=p_pairs[:, :nb, 1, :],
                 op=MAX,
@@ -185,12 +213,12 @@ def tile_gmpahead_pa_kernel(tc, pooled, p, Wout, out):
             cols = nb * CHANNELS
             feat = work.tile([P, GROUP * CHANNELS], F32)
             nc.vector.tensor_tensor(
-                out=feat[:, :cols], in0=kept[r]["y_leaky"][:, :cols], in1=kept[r]["p_max"][:, :cols], op=ADD
+                out=feat[:, :cols],
+                in0=kept[r]["y_leaky"][:, :cols],
+                in1=kept[r]["p_max"][:, :cols],
+                op=ADD,
             )
-            nc.sync.dma_start(
-                out=out[first : first + nb].rearrange("n b c -> b n c"),
-                in_=feat[:, :cols].rearrange("b (n c) -> b n c", n=nb),
-            )
+            nc.sync.dma_start(out=rows_of(r, out_rows), in_=feat[:, :cols])
 
         def run(stage, r):
             if 0 <= r < ROUNDS:

@@ -34,8 +34,7 @@ X_SETS = 2
 RUN = 4
 W_COLS_SCALAR = 176
 
-AHEAD = 2
-P_LATER = 2
+AHEAD = 3
 
 FLOPS = 2 * BINS * SAMPLES * K * CHANNELS
 
@@ -76,11 +75,15 @@ def tile_gmpahead_pa_kernel(tc, pooled, p, Wout, out):
                 "(i j) w -> i (j w)", j=nb
             )
 
-        def fetch_operands(r):
+        def fetch_pooled(r):
             first, nb = bins_of(r)
-            units = nb * PASSES
             x_raw = loads.tile([P, GROUP * K], BF16)
             nc.sync.dma_start(out=x_raw[:, : nb * K], in_=rows_of(r, pooled_rows))
+            kept[r] = {"x_raw": x_raw}
+
+        def fetch_weights(r):
+            first, nb = bins_of(r)
+            units = nb * PASSES
             w_raw = loads.tile([P, UNITS * PACK * CHANNELS], BF16)
             nc.sync.dma_start(
                 out=w_raw[:, : units * PACK * CHANNELS].rearrange("q (s f) -> q s f", s=units),
@@ -88,7 +91,7 @@ def tile_gmpahead_pa_kernel(tc, pooled, p, Wout, out):
                     "n (g q t) c -> q (n g) (t c)", g=PASSES, t=PACK
                 ),
             )
-            kept[r] = {"x_raw": x_raw, "w_raw": w_raw}
+            kept[r]["w_raw"] = w_raw
 
         def fetch_frames(r):
             first, nb = bins_of(r)
@@ -96,26 +99,35 @@ def tile_gmpahead_pa_kernel(tc, pooled, p, Wout, out):
             nc.sync.dma_start(out=p_raw[:, : nb * FRAMES * CHANNELS], in_=rows_of(r, p_rows))
             kept[r]["p_raw"] = p_raw
 
-        def prepare(r):
+        def transpose_pooled(r):
             first, nb = bins_of(r)
-            units = nb * PASSES
-
             x_words = kept[r]["x_raw"][:].bitcast(F32).rearrange(
                 "i (j g q u) -> i j g u q", j=GROUP, g=PASSES, u=WORDS
             )
-            x_grouped = work.tile([P, GROUP * K], BF16, align_bytes=64)
-            x_grouped_words = x_grouped[:].bitcast(F32).rearrange(
-                "q (j g i u) -> q j g i u", j=GROUP, g=PASSES, u=WORDS
-            )
+            kept[r]["x_turned"] = []
             for j in range(nb):
                 xt = xt_banks.tile([P, PASSES, WORDS, P], F32)
                 for g in range(PASSES):
                     for u in range(WORDS):
                         nc.tensor.transpose(xt[:, g, u, :], x_words[:, j, g, u, :], identity[:])
-                nc.scalar.copy(
-                    out=x_grouped_words[:, j], in_=xt[:].rearrange("q g u i -> q g i u")
-                )
+                kept[r]["x_turned"].append(xt)
 
+        def group_pooled(r):
+            first, nb = bins_of(r)
+            x_grouped = work.tile([P, GROUP * K], BF16, align_bytes=64)
+            x_grouped_words = x_grouped[:].bitcast(F32).rearrange(
+                "q (j g i u) -> q j g i u", j=GROUP, g=PASSES, u=WORDS
+            )
+            for j in range(nb):
+                nc.scalar.copy(
+                    out=x_grouped_words[:, j],
+                    in_=kept[r]["x_turned"][j][:].rearrange("q g u i -> q g i u"),
+                )
+            kept[r]["x_grouped"] = x_grouped
+
+        def group_weights(r):
+            first, nb = bins_of(r)
+            units = nb * PASSES
             w_grouped = work.tile([P, UNITS * CHANNELS * PACK], BF16, align_bytes=64)
             w_from = kept[r]["w_raw"][:].rearrange(
                 "q (s t c i) -> q s c t i", s=UNITS, t=PACK, i=RUN
@@ -125,34 +137,38 @@ def tile_gmpahead_pa_kernel(tc, pooled, p, Wout, out):
             for s in range(units):
                 nc.scalar.copy(out=w_to[:, s, :split], in_=w_from[:, s, :split])
             nc.vector.tensor_copy(out=w_to[:, :units, split:], in_=w_from[:, :units, split:])
-            kept[r]["x_grouped"] = x_grouped
             kept[r]["w_grouped"] = w_grouped
 
-        def multiply(r):
+        def quantise_pooled(r):
             first, nb = bins_of(r)
-            units = nb * PASSES
             share = P // nb
-
-            x_codes = x_code_sets[r % X_SETS]
-            x_scales = x_scale_sets[r % X_SETS]
-            for s in range(units):
+            for s in range(nb * PASSES):
                 for n in range(nb):
                     filled = slice(s * X_SLOT + n * P, s * X_SLOT + n * P + share)
                     nc.vector.quantize_mx(
-                        out=x_codes[:, filled].bitcast(FP8X4),
-                        scales=x_scales[:, filled],
+                        out=x_code_sets[r % X_SETS][:, filled].bitcast(FP8X4),
+                        scales=x_scale_sets[r % X_SETS][:, filled],
                         in_=kept[r]["x_grouped"][
                             :, (s * P + n * share) * PACK : (s * P + (n + 1) * share) * PACK
                         ],
                     )
+
+        def quantise_weights(r):
+            first, nb = bins_of(r)
+            cols = nb * PASSES * CHANNELS
             w_codes = work.tile([P, UNITS * CHANNELS], U32, align_bytes=64)
             w_scales = work.tile([P, UNITS * CHANNELS], U8, align_bytes=64)
             nc.vector.quantize_mx(
-                out=w_codes[:, : units * CHANNELS].bitcast(FP8X4),
-                scales=w_scales[:, : units * CHANNELS],
-                in_=kept[r]["w_grouped"][:, : units * CHANNELS * PACK],
+                out=w_codes[:, :cols].bitcast(FP8X4),
+                scales=w_scales[:, :cols],
+                in_=kept[r]["w_grouped"][:, : cols * PACK],
             )
+            kept[r]["w_codes"] = w_codes
+            kept[r]["w_scales"] = w_scales
 
+        def multiply(r):
+            first, nb = bins_of(r)
+            share = P // nb
             y = y_banks.tile([P, GROUP * CHANNELS], F32)
             for j in range(nb):
                 for n in range(nb):
@@ -163,25 +179,36 @@ def tile_gmpahead_pa_kernel(tc, pooled, p, Wout, out):
                         w_cols = slice(w_start, w_start + CHANNELS)
                         nc.tensor.matmul_mx(
                             out=y[:, j * CHANNELS : (j + 1) * CHANNELS],
-                            lhsT=x_codes[:, x_cols].bitcast(FP8X4),
-                            lhsT_scale=x_scales[:, x_cols],
-                            rhs=w_codes[:, w_cols].bitcast(FP8X4),
-                            rhs_scale=w_scales[:, w_cols],
+                            lhsT=x_code_sets[r % X_SETS][:, x_cols].bitcast(FP8X4),
+                            lhsT_scale=x_scale_sets[r % X_SETS][:, x_cols],
+                            rhs=kept[r]["w_codes"][:, w_cols].bitcast(FP8X4),
+                            rhs_scale=kept[r]["w_scales"][:, w_cols],
                             start=(n == 0 and g == 0),
                             stop=(n == nb - 1 and g == PASSES - 1),
                         )
-
-            y_small = work.tile([P, GROUP * CHANNELS], F32)
-            nc.scalar.mul(
-                out=y_small[:, : nb * CHANNELS], in_=y[:, : nb * CHANNELS], mul=LEAKY_SLOPE
-            )
             kept[r]["y"] = y
-            kept[r]["y_small"] = y_small
 
-        def relu(r):
+        def shrink(r):
             first, nb = bins_of(r)
             cols = nb * CHANNELS
+            y_small = work.tile([P, GROUP * CHANNELS], F32)
+            nc.scalar.mul(out=y_small[:, :cols], in_=kept[r]["y"][:, :cols], mul=LEAKY_SLOPE)
+            kept[r]["y_small"] = y_small
 
+        def leaky_relu(r):
+            first, nb = bins_of(r)
+            cols = nb * CHANNELS
+            y_leaky = work.tile([P, GROUP * CHANNELS], F32)
+            nc.vector.tensor_tensor(
+                out=y_leaky[:, :cols],
+                in0=kept[r]["y"][:, :cols],
+                in1=kept[r]["y_small"][:, :cols],
+                op=MAX,
+            )
+            kept[r]["y_leaky"] = y_leaky
+
+        def max_of_frame_pairs(r):
+            first, nb = bins_of(r)
             p_halves = kept[r]["p_raw"][:].rearrange("i (j h f) -> i j h f", j=GROUP, h=2)
             p_half = work.tile([P, GROUP * 2 * CHANNELS], BF16)
             nc.vector.tensor_tensor(
@@ -190,14 +217,11 @@ def tile_gmpahead_pa_kernel(tc, pooled, p, Wout, out):
                 in1=p_halves[:, :nb, 1, :],
                 op=MAX,
             )
-            y_leaky = work.tile([P, GROUP * CHANNELS], F32)
-            nc.vector.tensor_tensor(
-                out=y_leaky[:, :cols],
-                in0=kept[r]["y"][:, :cols],
-                in1=kept[r]["y_small"][:, :cols],
-                op=MAX,
-            )
-            p_pairs = p_half[:].rearrange("i (j h c) -> i j h c", j=GROUP, h=2)
+            kept[r]["p_half"] = p_half
+
+        def max_of_frames(r):
+            first, nb = bins_of(r)
+            p_pairs = kept[r]["p_half"][:].rearrange("i (j h c) -> i j h c", j=GROUP, h=2)
             p_max = work.tile([P, GROUP * CHANNELS], BF16)
             nc.vector.tensor_tensor(
                 out=p_max[:].rearrange("i (j c) -> i j c", j=GROUP)[:, :nb],
@@ -205,7 +229,6 @@ def tile_gmpahead_pa_kernel(tc, pooled, p, Wout, out):
                 in1=p_pairs[:, :nb, 1, :],
                 op=MAX,
             )
-            kept[r]["y_leaky"] = y_leaky
             kept[r]["p_max"] = p_max
 
         def finish(r):
@@ -226,9 +249,18 @@ def tile_gmpahead_pa_kernel(tc, pooled, p, Wout, out):
 
         with tc.manual_schedule():
             for step in range(ROUNDS + AHEAD + 3):
-                run(fetch_operands, step)
-                run(fetch_frames, step - P_LATER)
-                run(prepare, step - AHEAD)
-                run(multiply, step - AHEAD - 1)
-                run(relu, step - AHEAD - 2)
-                run(finish, step - AHEAD - 3)
+                r = step - AHEAD - 1
+                run(fetch_pooled, step)
+                run(fetch_weights, step - 1)
+                run(fetch_frames, step - 2)
+                run(transpose_pooled, r + 1)
+                run(group_weights, r)
+                run(finish, r - 2)
+                run(max_of_frame_pairs, r - 1)
+                run(quantise_pooled, r)
+                run(max_of_frames, r - 1)
+                run(quantise_weights, r)
+                run(multiply, r)
+                run(shrink, r - 1)
+                run(leaky_relu, r - 1)
+                run(group_pooled, r + 1)

@@ -32,7 +32,7 @@ X_SLOT = P * (GROUP - 1) + P // GROUP
 X_SETS = 2
 
 RUN = 4
-W_COLS_SCALAR = 176
+W_COLS_SCALAR = 160
 
 AHEAD = 3
 
@@ -250,9 +250,9 @@ def tile_gmpahead_pa_kernel(tc, pooled, p, Wout, out):
         with tc.manual_schedule():
             for step in range(ROUNDS + AHEAD + 3):
                 r = step - AHEAD - 1
-                run(fetch_pooled, step)
                 run(fetch_weights, step - 1)
                 run(fetch_frames, step - 2)
+                run(fetch_pooled, step)
                 run(transpose_pooled, r + 1)
                 run(group_weights, r)
                 run(finish, r - 2)

@@ -36,6 +36,8 @@ W_COLS_SCALAR = 160
 
 AHEAD = 3
 
+STORE_LAG = 3
+
 FLOPS = 2 * BINS * SAMPLES * K * CHANNELS
 
 
@@ -47,7 +49,9 @@ def tile_gmpahead_pa_kernel(tc, pooled, p, Wout, out):
 
     with tc.tile_pool(name="const", bufs=1) as const, tc.tile_pool(
         name="loads", bufs=AHEAD + 2
-    ) as loads, tc.tile_pool(name="work", bufs=3) as work, tc.psum_pool(
+    ) as loads, tc.tile_pool(name="work", bufs=3) as work, tc.tile_pool(
+        name="results", bufs=STORE_LAG + 3
+    ) as results, tc.psum_pool(
         name="xt_banks", bufs=2 * GROUP
     ) as xt_banks, tc.psum_pool(name="y_banks", bufs=3) as y_banks:
         identity = const.tile([P, P], F32)
@@ -234,25 +238,30 @@ def tile_gmpahead_pa_kernel(tc, pooled, p, Wout, out):
         def finish(r):
             first, nb = bins_of(r)
             cols = nb * CHANNELS
-            feat = work.tile([P, GROUP * CHANNELS], F32)
+            feat = results.tile([P, GROUP * CHANNELS], F32)
             nc.vector.tensor_tensor(
                 out=feat[:, :cols],
                 in0=kept[r]["y_leaky"][:, :cols],
                 in1=kept[r]["p_max"][:, :cols],
                 op=ADD,
             )
-            nc.sync.dma_start(out=rows_of(r, out_rows), in_=feat[:, :cols])
+            kept[r]["feat"] = feat
+
+        def store(r):
+            first, nb = bins_of(r)
+            nc.sync.dma_start(out=rows_of(r, out_rows), in_=kept[r]["feat"][:, : nb * CHANNELS])
 
         def run(stage, r):
             if 0 <= r < ROUNDS:
                 stage(r)
 
         with tc.manual_schedule():
-            for step in range(ROUNDS + AHEAD + 3):
+            for step in range(ROUNDS + AHEAD + 3 + STORE_LAG):
                 r = step - AHEAD - 1
                 run(fetch_weights, step - 1)
                 run(fetch_frames, step - 2)
                 run(fetch_pooled, step)
+                run(store, r - 2 - STORE_LAG)
                 run(transpose_pooled, r + 1)
                 run(group_weights, r)
                 run(finish, r - 2)

@@ -36,7 +36,7 @@ W_COLS_SCALAR = 160
 
 AHEAD = 3
 
-STORE_LAG = 3
+STORE_LAG = 6
 
 FLOPS = 2 * BINS * SAMPLES * K * CHANNELS
 

@@ -36,7 +36,7 @@ W_COLS_SCALAR = 160
 
 AHEAD = 3
 
-STORE_LAG = 6
+STORE_LAG = 12
 
 FLOPS = 2 * BINS * SAMPLES * K * CHANNELS
 

@@ -32,7 +32,7 @@ X_SLOT = P * (GROUP - 1) + P // GROUP
 X_SETS = 2
 
 RUN = 4
-W_COLS_SCALAR = 160
+W_COLS_SCALAR = 168
 
 AHEAD = 3
 
@@ -83,19 +83,21 @@ def tile_gmpahead_pa_kernel(tc, pooled, p, Wout, out):
             first, nb = bins_of(r)
             x_raw = loads.tile([P, GROUP * K], BF16)
             nc.sync.dma_start(out=x_raw[:, : nb * K], in_=rows_of(r, pooled_rows))
-            kept[r] = {"x_raw": x_raw}
+            kept.setdefault(r, {})["x_raw"] = x_raw
 
         def fetch_weights(r):
             first, nb = bins_of(r)
             units = nb * PASSES
             w_raw = loads.tile([P, UNITS * PACK * CHANNELS], BF16)
-            nc.sync.dma_start(
-                out=w_raw[:, : units * PACK * CHANNELS].rearrange("q (s f) -> q s f", s=units),
-                in_=Wout[first : first + nb].rearrange(
-                    "n (g q t) c -> q (n g) (t c)", g=PASSES, t=PACK
-                ),
+            w_to = w_raw[:, : units * PACK * CHANNELS].rearrange("q (s f) -> q s f", s=units)
+            w_from = Wout[first : first + nb].rearrange(
+                "n (g q t) c -> q (n g) (t c)", g=PASSES, t=PACK
             )
-            kept[r]["w_raw"] = w_raw
+            pieces = units if r == 0 else 1
+            for i in range(pieces):
+                part = slice(i * units // pieces, (i + 1) * units // pieces)
+                nc.sync.dma_start(out=w_to[:, part], in_=w_from[:, part])
+            kept.setdefault(r, {})["w_raw"] = w_raw
 
         def fetch_frames(r):
             first, nb = bins_of(r)
@@ -258,12 +260,17 @@ def tile_gmpahead_pa_kernel(tc, pooled, p, Wout, out):
         with tc.manual_schedule():
             for step in range(ROUNDS + AHEAD + 3 + STORE_LAG):
                 r = step - AHEAD - 1
-                run(fetch_weights, step - 1)
+                if step == 0:
+                    fetch_weights(0)
+                if step > 1:
+                    run(fetch_weights, step - 1)
                 run(fetch_frames, step - 2)
                 run(fetch_pooled, step)
                 run(store, r - 2 - STORE_LAG)
                 run(transpose_pooled, r + 1)
                 run(group_weights, r)
+                if r == 0:
+                    group_pooled(0)
                 run(finish, r - 2)
                 run(max_of_frame_pairs, r - 1)
                 run(quantise_pooled, r)
@@ -272,4 +279,5 @@ def tile_gmpahead_pa_kernel(tc, pooled, p, Wout, out):
                 run(multiply, r)
                 run(shrink, r - 1)
                 run(leaky_relu, r - 1)
-                run(group_pooled, r + 1)
+                if r + 1 > 0:
+                    run(group_pooled, r + 1)

@@ -31,7 +31,7 @@ UNITS = GROUP * PASSES
 X_SLOT = P * (GROUP - 1) + P // GROUP
 X_SETS = 2
 
-RUN = 4
+RUN = 8
 W_COLS_SCALAR = 168
 
 AHEAD = 3

@@ -93,7 +93,7 @@ def tile_gmpahead_pa_kernel(tc, pooled, p, Wout, out):
             w_from = Wout[first : first + nb].rearrange(
                 "n (g q t) c -> q (n g) (t c)", g=PASSES, t=PACK
             )
-            pieces = units if r == 0 else 1
+            pieces = units if r <= 1 else 1
             for i in range(pieces):
                 part = slice(i * units // pieces, (i + 1) * units // pieces)
                 nc.sync.dma_start(out=w_to[:, part], in_=w_from[:, part])
@@ -164,11 +164,13 @@ def tile_gmpahead_pa_kernel(tc, pooled, p, Wout, out):
             cols = nb * PASSES * CHANNELS
             w_codes = work.tile([P, UNITS * CHANNELS], U32, align_bytes=64)
             w_scales = work.tile([P, UNITS * CHANNELS], U8, align_bytes=64)
-            nc.vector.quantize_mx(
-                out=w_codes[:, :cols].bitcast(FP8X4),
-                scales=w_scales[:, :cols],
-                in_=kept[r]["w_grouped"][:, : cols * PACK],
-            )
+            for n in range(nb):
+                part = slice(n * cols // nb, (n + 1) * cols // nb)
+                nc.vector.quantize_mx(
+                    out=w_codes[:, part].bitcast(FP8X4),
+                    scales=w_scales[:, part],
+                    in_=kept[r]["w_grouped"][:, n * cols // nb * PACK : (n + 1) * cols // nb * PACK],
+                )
             kept[r]["w_codes"] = w_codes
             kept[r]["w_scales"] = w_scales
 
@@ -269,15 +271,18 @@ def tile_gmpahead_pa_kernel(tc, pooled, p, Wout, out):
                 run(store, r - 2 - STORE_LAG)
                 run(transpose_pooled, r + 1)
                 run(group_weights, r)
-                if r == 0:
-                    group_pooled(0)
+                if 0 <= r <= 1:
+                    group_pooled(r)
                 run(finish, r - 2)
                 run(max_of_frame_pairs, r - 1)
+                if 0 <= r <= 1:
+                    quantise_weights(r)
                 run(quantise_pooled, r)
                 run(max_of_frames, r - 1)
-                run(quantise_weights, r)
+                if r > 1:
+                    run(quantise_weights, r)
                 run(multiply, r)
                 run(shrink, r - 1)
                 run(leaky_relu, r - 1)
-                if r + 1 > 0:
+                if r + 1 > 1:
                     run(group_pooled, r + 1)

@@ -93,7 +93,7 @@ def tile_gmpahead_pa_kernel(tc, pooled, p, Wout, out):
             w_from = Wout[first : first + nb].rearrange(
                 "n (g q t) c -> q (n g) (t c)", g=PASSES, t=PACK
             )
-            pieces = units if r <= 1 else 1
+            pieces = units
             for i in range(pieces):
                 part = slice(i * units // pieces, (i + 1) * units // pieces)
                 nc.sync.dma_start(out=w_to[:, part], in_=w_from[:, part])

import concourse.mybir as mybir
from concourse.masks import make_identity

BF16 = mybir.dt.bfloat16
F32 = mybir.dt.float32
I32 = mybir.dt.int32
U32 = mybir.dt.uint32
U8 = mybir.dt.uint8
FP8X4 = mybir.dt.float8_e4m3fn_x4
MAX = mybir.AluOpType.max
ADD = mybir.AluOpType.add

BINS = 31
SAMPLES = 128
FRAMES = 4
CHANNELS = 256
K = 1024
LEAKY_SLOPE = 0.01

P = 128
PACK = 4
K_PASS = P * PACK
PASSES = K // K_PASS
PAIR = 2
WORDS = PACK // PAIR

GROUP = 2
ROUNDS = (BINS + GROUP - 1) // GROUP
UNITS = GROUP * PASSES

X_SLOT = P * (GROUP - 1) + P // GROUP
X_SETS = 2

RUN = 8
W_COLS_SCALAR = 168

AHEAD = 3

STORE_LAG = 12

FLOPS = 2 * BINS * SAMPLES * K * CHANNELS


def tile_gmpahead_pa_kernel(tc, pooled, p, Wout, out):
    nc = tc.nc
    pooled_rows = pooled.rearrange("n b k -> (n b) k")
    p_rows = p.rearrange("n b t c -> (n b) (t c)")
    out_rows = out.rearrange("n b c -> (n b) c")

    with tc.tile_pool(name="const", bufs=1) as const, tc.tile_pool(
        name="loads", bufs=AHEAD + 2
    ) as loads, tc.tile_pool(name="work", bufs=3) as work, tc.tile_pool(
        name="results", bufs=STORE_LAG + 3
    ) as results, tc.psum_pool(
        name="xt_banks", bufs=2 * GROUP
    ) as xt_banks, tc.psum_pool(name="y_banks", bufs=3) as y_banks:
        identity = const.tile([P, P], F32)
        make_identity(nc, identity[:])

        x_code_sets = []
        x_scale_sets = []
        for i in range(X_SETS):
            x_codes = const.tile([P, UNITS * X_SLOT], U32, align_bytes=64, name="x_codes_%d" % i)
            x_scales = const.tile([P, UNITS * X_SLOT], U8, align_bytes=64, name="x_scales_%d" % i)
            nc.vector.memset(x_codes[:].bitcast(I32), 0)
            nc.vector.memset(x_scales[:].bitcast(I32), 0)
            x_code_sets.append(x_codes)
            x_scale_sets.append(x_scales)

        kept = {}

        def bins_of(r):
            first = r * GROUP
            return first, min(GROUP, BINS - first)

        def rows_of(r, dram_rows):
            first, nb = bins_of(r)
            return dram_rows[first * SAMPLES : (first + nb) * SAMPLES, :].rearrange(
                "(i j) w -> i (j w)", j=nb
            )

        def fetch_pooled(r):
            first, nb = bins_of(r)
            x_raw = loads.tile([P, GROUP * K], BF16)
            nc.sync.dma_start(out=x_raw[:, : nb * K], in_=rows_of(r, pooled_rows))
            kept.setdefault(r, {})["x_raw"] = x_raw

        def fetch_weights(r):
            first, nb = bins_of(r)
            units = nb * PASSES
            w_raw = loads.tile([P, UNITS * PACK * CHANNELS], BF16)
            w_to = w_raw[:, : units * PACK * CHANNELS].rearrange("q (s f) -> q s f", s=units)
            w_from = Wout[first : first + nb].rearrange(
                "n (g q t) c -> q (n g) (t c)", g=PASSES, t=PACK
            )
            pieces = units
            for i in range(pieces):
                part = slice(i * units // pieces, (i + 1) * units // pieces)
                nc.sync.dma_start(out=w_to[:, part], in_=w_from[:, part])
            kept.setdefault(r, {})["w_raw"] = w_raw

        def fetch_frames(r):
            first, nb = bins_of(r)
            p_raw = loads.tile([P, GROUP * FRAMES * CHANNELS], BF16)
            nc.sync.dma_start(out=p_raw[:, : nb * FRAMES * CHANNELS], in_=rows_of(r, p_rows))
            kept[r]["p_raw"] = p_raw

        def transpose_pooled(r):
            first, nb = bins_of(r)
            x_words = kept[r]["x_raw"][:].bitcast(F32).rearrange(
                "i (j g q u) -> i j g u q", j=GROUP, g=PASSES, u=WORDS
            )
            kept[r]["x_turned"] = []
            for j in range(nb):
                xt = xt_banks.tile([P, PASSES, WORDS, P], F32)
                for g in range(PASSES):
                    for u in range(WORDS):
                        nc.tensor.transpose(xt[:, g, u, :], x_words[:, j, g, u, :], identity[:])
                kept[r]["x_turned"].append(xt)

        def group_pooled(r):
            first, nb = bins_of(r)
            x_grouped = work.tile([P, GROUP * K], BF16, align_bytes=64)
            x_grouped_words = x_grouped[:].bitcast(F32).rearrange(
                "q (j g i u) -> q j g i u", j=GROUP, g=PASSES, u=WORDS
            )
            for j in range(nb):
                nc.scalar.copy(
                    out=x_grouped_words[:, j],
                    in_=kept[r]["x_turned"][j][:].rearrange("q g u i -> q g i u"),
                )
            kept[r]["x_grouped"] = x_grouped

        def group_weights(r):
            first, nb = bins_of(r)
            units = nb * PASSES
            w_grouped = work.tile([P, UNITS * CHANNELS * PACK], BF16, align_bytes=64)
            w_from = kept[r]["w_raw"][:].rearrange(
                "q (s t c i) -> q s c t i", s=UNITS, t=PACK, i=RUN
            )
            w_to = w_grouped[:].rearrange("q (s c i t) -> q s c t i", s=UNITS, t=PACK, i=RUN)
            split = W_COLS_SCALAR // RUN
            for s in range(units):
                nc.scalar.copy(out=w_to[:, s, :split], in_=w_from[:, s, :split])
            nc.vector.tensor_copy(out=w_to[:, :units, split:], in_=w_from[:, :units, split:])
            kept[r]["w_grouped"] = w_grouped

        def quantise_pooled(r):
            first, nb = bins_of(r)
            share = P // nb
            for s in range(nb * PASSES):
                for n in range(nb):
                    filled = slice(s * X_SLOT + n * P, s * X_SLOT + n * P + share)
                    nc.vector.quantize_mx(
                        out=x_code_sets[r % X_SETS][:, filled].bitcast(FP8X4),
                        scales=x_scale_sets[r % X_SETS][:, filled],
                        in_=kept[r]["x_grouped"][
                            :, (s * P + n * share) * PACK : (s * P + (n + 1) * share) * PACK
                        ],
                    )

        def quantise_weights(r):
            first, nb = bins_of(r)
            cols = nb * PASSES * CHANNELS
            w_codes = work.tile([P, UNITS * CHANNELS], U32, align_bytes=64)
            w_scales = work.tile([P, UNITS * CHANNELS], U8, align_bytes=64)
            for n in range(nb):
                part = slice(n * cols // nb, (n + 1) * cols // nb)
                nc.vector.quantize_mx(
                    out=w_codes[:, part].bitcast(FP8X4),
                    scales=w_scales[:, part],
                    in_=kept[r]["w_grouped"][:, n * cols // nb * PACK : (n + 1) * cols // nb * PACK],
                )
            kept[r]["w_codes"] = w_codes
            kept[r]["w_scales"] = w_scales

        def multiply(r):
            first, nb = bins_of(r)
            share = P // nb
            y = y_banks.tile([P, GROUP * CHANNELS], F32)
            for j in range(nb):
                for n in range(nb):
                    for g in range(PASSES):
                        x_start = (j * PASSES + g) * X_SLOT + n * share
                        x_cols = slice(x_start, x_start + P)
                        w_start = (n * PASSES + g) * CHANNELS
                        w_cols = slice(w_start, w_start + CHANNELS)
                        nc.tensor.matmul_mx(
                            out=y[:, j * CHANNELS : (j + 1) * CHANNELS],
                            lhsT=x_code_sets[r % X_SETS][:, x_cols].bitcast(FP8X4),
                            lhsT_scale=x_scale_sets[r % X_SETS][:, x_cols],
                            rhs=kept[r]["w_codes"][:, w_cols].bitcast(FP8X4),
                            rhs_scale=kept[r]["w_scales"][:, w_cols],
                            start=(n == 0 and g == 0),
                            stop=(n == nb - 1 and g == PASSES - 1),
                        )
            kept[r]["y"] = y

        def shrink(r):
            first, nb = bins_of(r)
            cols = nb * CHANNELS
            y_small = work.tile([P, GROUP * CHANNELS], F32)
            nc.scalar.mul(out=y_small[:, :cols], in_=kept[r]["y"][:, :cols], mul=LEAKY_SLOPE)
            kept[r]["y_small"] = y_small

        def leaky_relu(r):
            first, nb = bins_of(r)
            cols = nb * CHANNELS
            y_leaky = work.tile([P, GROUP * CHANNELS], F32)
            nc.vector.tensor_tensor(
                out=y_leaky[:, :cols],
                in0=kept[r]["y"][:, :cols],
                in1=kept[r]["y_small"][:, :cols],
                op=MAX,
            )
            kept[r]["y_leaky"] = y_leaky

        def max_of_frame_pairs(r):
            first, nb = bins_of(r)
            p_halves = kept[r]["p_raw"][:].rearrange("i (j h f) -> i j h f", j=GROUP, h=2)
            p_half = work.tile([P, GROUP * 2 * CHANNELS], BF16)
            nc.vector.tensor_tensor(
                out=p_half[:].rearrange("i (j f) -> i j f", j=GROUP)[:, :nb],
                in0=p_halves[:, :nb, 0, :],
                in1=p_halves[:, :nb, 1, :],
                op=MAX,
            )
            kept[r]["p_half"] = p_half

        def max_of_frames(r):
            first, nb = bins_of(r)
            p_pairs = kept[r]["p_half"][:].rearrange("i (j h c) -> i j h c", j=GROUP, h=2)
            p_max = work.tile([P, GROUP * CHANNELS], BF16)
            nc.vector.tensor_tensor(
                out=p_max[:].rearrange("i (j c) -> i j c", j=GROUP)[:, :nb],
                in0=p_pairs[:, :nb, 0, :],
                in1=p_pairs[:, :nb, 1, :],
                op=MAX,
            )
            kept[r]["p_max"] = p_max

        def finish(r):
            first, nb = bins_of(r)
            cols = nb * CHANNELS
            feat = results.tile([P, GROUP * CHANNELS], F32)
            nc.vector.tensor_tensor(
                out=feat[:, :cols],
                in0=kept[r]["y_leaky"][:, :cols],
                in1=kept[r]["p_max"][:, :cols],
                op=ADD,
            )
            kept[r]["feat"] = feat

        def store(r):
            first, nb = bins_of(r)
            nc.sync.dma_start(out=rows_of(r, out_rows), in_=kept[r]["feat"][:, : nb * CHANNELS])

        def run(stage, r):
            if 0 <= r < ROUNDS:
                stage(r)

        with tc.manual_schedule():
            for step in range(ROUNDS + AHEAD + 3 + STORE_LAG):
                r = step - AHEAD - 1
                if step == 0:
                    fetch_weights(0)
                if step > 1:
                    run(fetch_weights, step - 1)
                run(fetch_frames, step - 2)
                run(fetch_pooled, step)
                run(store, r - 2 - STORE_LAG)
                run(transpose_pooled, r + 1)
                run(group_weights, r)
                if 0 <= r <= 1:
                    group_pooled(r)
                run(finish, r - 2)
                run(max_of_frame_pairs, r - 1)
                if 0 <= r <= 1:
                    quantise_weights(r)
                run(quantise_pooled, r)
                run(max_of_frames, r - 1)
                if r > 1:
                    run(quantise_weights, r)
                run(multiply, r)
                run(shrink, r - 1)
                run(leaky_relu, r - 1)
                if r + 1 > 1:
                    run(group_pooled, r + 1)
